import numpy as np
import ml_dtypes


def mxq(x, axis, fmt="e4m3"):
    dtype, down = {"e4m3": (ml_dtypes.float8_e4m3fn, 7), "e5m2": (ml_dtypes.float8_e5m2, 14)}[fmt]
    v = np.moveaxis(np.asarray(x, np.float32).astype(ml_dtypes.bfloat16).astype(np.float64), axis, -1)
    blocks = v.reshape(v.shape[:-1] + (-1, 32))
    amax = np.abs(blocks).max(-1, keepdims=True)
    byte = np.maximum(np.where(amax > 0, np.frexp(amax)[1] - 1 + 127, 0) - down, 1)
    scale = np.exp2(byte - 127.0)
    codes = (blocks / scale).astype(np.float32).astype(dtype).astype(np.float64)
    return np.moveaxis((codes * scale).reshape(v.shape), -1, axis)


WIDE = False


def mx_kscale(k):
    if not WIDE:
        return np.ones(k)
    levels = np.array([10, -10, 5, -5, 0])
    a = np.random.permutation(np.resize(levels, k // 512 * 4)).reshape(k // 512, 4)
    idx = np.arange(k)
    return np.exp2(a[idx // 512, idx % 128 // 32])


BF16 = ml_dtypes.bfloat16


def bf(x):
    return np.asarray(x, np.float32).astype(BF16)


def f64(x):
    return np.asarray(x).astype(np.float64)


B, L, H = 8, 512, 512
MASK_VALUE = -3.4028234663852886e38


def setup_inputs():
    s, t = mx_kscale(H), mx_kscale(H)
    qs = np.sqrt(1.5) * H ** 0.25
    q0 = np.random.standard_normal((B, L, H)) * qs
    k0 = np.random.standard_normal((B, L, H)) * qs + q0 * (5.0 / qs ** 2)
    return {"q": bf(q0 * s), "k": bf(k0 / s),
            "x": bf(np.random.standard_normal((B, L, H)) * t),
            "Wv": bf(np.random.standard_normal((H, H)) * 2.0 / np.sqrt(H) / t[None, :]),
            "bv": bf(np.random.standard_normal(H) * 0.1)}


def reference(q, k, x, Wv, bv):
    v = (mxq(f64(x), 2, "e4m3") @ mxq(f64(Wv), 1, "e4m3").T) + f64(bv)
    a = (mxq(f64(q), 2, "e4m3") @ mxq(f64(k), 2, "e4m3").transpose(0, 2, 1)) / H
    own = np.arange(L)[:, None] == np.arange(L)[None, :]
    a = np.where(own[None, :, :], MASK_VALUE, a)
    e = np.exp(a - a.max(-1, keepdims=True))
    return (mxq(e, 2, "e4m3") @ mxq(v, 1, "e4m3")) / e.sum(-1, keepdims=True)

@@ -1,0 +1,258 @@
+from contextlib import ExitStack
+
+import concourse.mybir as mybir
+from concourse.masks import make_identity
+
+F32 = mybir.dt.float32
+BF16 = mybir.dt.bfloat16
+U32 = mybir.dt.uint32
+U8 = mybir.dt.uint8
+FP8X4 = mybir.dt.float8_e4m3fn_x4
+ALU = mybir.AluOpType
+ACT = mybir.ActivationFunctionType
+
+P = 128
+PACK = 4
+B, L, H = 8, 512, 512
+TILES = L // P
+WORDS = H // 2
+MASK_VALUE = -3.4028234663852886e38
+LOADS_AHEAD = 4
+
+FLOPS = 3 * 2 * B * L * H * H
+
+
+def tile_scaleddotproductattention_pa_t_kernel(tc, q, k, x, Wv, bv, out):
+    nc = tc.nc
+    with ExitStack() as ctx:
+        const = ctx.enter_context(tc.tile_pool(name="const", bufs=1))
+        raw = ctx.enter_context(tc.tile_pool(name="raw", bufs=LOADS_AHEAD))
+        work = ctx.enter_context(tc.tile_pool(name="work", bufs=2))
+        results = ctx.enter_context(tc.tile_pool(name="results", bufs=3))
+        flip_banks = ctx.enter_context(tc.psum_pool(name="flip_banks", bufs=3))
+        prod_banks = ctx.enter_context(tc.psum_pool(name="prod_banks", bufs=5))
+        ctx.enter_context(tc.manual_schedule())
+
+        def load(pool, rows, name):
+            tile = pool.tile([P, TILES * H], BF16, name=name, tag=name)
+            nc.sync.dma_start(
+                out=tile[:].rearrange("p (s f) -> p s f", s=TILES),
+                in_=rows.rearrange("(s p) f -> p s f", p=P),
+            )
+            return tile
+
+        def load_paired(pool, rows, name):
+            tile = pool.tile([P, TILES * H], BF16, name=name, tag=name)
+            nc.sync.dma_start(
+                out=tile[:].rearrange("p (u e f) -> p u e f", u=2, e=2),
+                in_=rows.rearrange("(u p e) f -> p u e f", u=2, e=2),
+            )
+            return tile
+
+        def load_entry(b):
+            inputs[b] = {
+                "x": load_paired(raw, x[b, :, :], "x_raw"),
+                "k": load(raw, k[b, :, :], "k_raw"),
+                "q": load(raw, q[b, :, :], "q_raw"),
+            }
+
+        def mx_operand(pool, name):
+            return {
+                "grouped": pool.tile([P, L * PACK], BF16, name=name + "_grouped", tag=name + "_grouped", align_bytes=64),
+                "codes": pool.tile([P, L], U32, name=name + "_codes", tag=name + "_codes", align_bytes=64),
+                "scales": pool.tile([P, L], U8, name=name + "_scales", tag=name + "_scales", align_bytes=64),
+            }
+
+        def flip_half(source, operand, half):
+            words = source[:].bitcast(F32).rearrange("p (s w) -> p s w", s=TILES)
+            bank = flip_banks.tile([P, 2, 2 * P], F32, name="flipped", tag="flipped")
+            for s in range(2):
+                for u in range(2):
+                    nc.tensor.transpose(
+                        bank[:, u, s * P : (s + 1) * P],
+                        words[:, 2 * half + s, u * P : (u + 1) * P],
+                        identity[:],
+                    )
+            pairs = operand["grouped"][:].bitcast(F32).rearrange("p (c u) -> p c u", u=2)
+            nc.scalar.copy(
+                out=pairs[:, half * 2 * P : (half + 1) * 2 * P, :],
+                in_=bank[:].rearrange("p u c -> p c u"),
+            )
+
+        def quantise(operand, first, count):
+            cols = slice(first, first + count)
+            nc.vector.quantize_mx(
+                out=operand["codes"][:, cols].bitcast(FP8X4),
+                scales=operand["scales"][:, cols],
+                in_=operand["grouped"][:, first * PACK : (first + count) * PACK],
+            )
+
+        def mx_pass(acc, stationary, s_first, moving, m_first, m_count):
+            s_cols = slice(s_first, s_first + P)
+            m_cols = slice(m_first, m_first + m_count)
+            nc.tensor.matmul_mx(
+                out=acc,
+                lhsT=stationary["codes"][:, s_cols].bitcast(FP8X4),
+                lhsT_scale=stationary["scales"][:, s_cols],
+                rhs=moving["codes"][:, m_cols].bitcast(FP8X4),
+                rhs_scale=moving["scales"][:, m_cols],
+                start=True,
+                stop=True,
+            )
+
+        def project(b):
+            v_banks[b] = []
+            for c in range(TILES):
+                bank = prod_banks.tile([P, TILES, P], F32, name="v_bank", tag="product")
+                for t in range(TILES):
+                    mx_pass(bank[:, t, :], ops[b]["x"], t * P, w_op, c * P, P)
+                v_banks[b].append(bank)
+
+        def add_bias(b, c):
+            feats = slice(c * P, (c + 1) * P)
+            grouped = ops[b]["v"]["grouped"][:].rearrange("p (h t) -> p h t", t=PACK)
+            nc.vector.tensor_tensor(
+                out=grouped[:, feats, :],
+                in0=v_banks[b][c][:].rearrange("p t h -> p h t"),
+                in1=bias[:, feats].unsqueeze(2).to_broadcast([P, P, PACK]),
+                op=ALU.add,
+            )
+
+        def scores(b):
+            a_banks[b] = []
+            for m in range(TILES):
+                bank = prod_banks.tile([P, L], F32, name="a_bank", tag="product")
+                mx_pass(bank[:], ops[b]["q"], m * P, ops[b]["k"], 0, L)
+                a_banks[b].append(bank)
+
+        def replace_diagonal(b, m):
+            nc.vector.tensor_tensor(
+                out=soft[b]["a"][:, m, :],
+                in0=a_banks[b][m][:],
+                in1=own_mask[:, (TILES - 1 - m) * P : (TILES - 1 - m) * P + L],
+                op=ALU.min,
+            )
+
+        def row_maximum(b, m):
+            nc.vector.tensor_scalar(
+                out=soft[b]["a"][:, m, :],
+                in0=soft[b]["a"][:, m, :],
+                scalar1=-1.0 / H,
+                scalar2=None,
+                op0=ALU.mult,
+                op1=ALU.min,
+                accum_out=soft[b]["neg_max"][:, m : m + 1],
+            )
+
+        def exponential(b, m):
+            nc.scalar.activation(
+                out=soft[b]["e"][:, m * L : (m + 1) * L],
+                in_=soft[b]["a"][:, m, :],
+                func=ACT.Exp,
+                bias=soft[b]["neg_max"][:, m : m + 1],
+                scale=-1.0,
+                accum_out=soft[b]["row_sum"][:, m : m + 1],
+            )
+
+        def mix(b, m):
+            bank = prod_banks.tile([P, H], F32, name="o_bank", tag="product")
+            mx_pass(bank[:], ops[b]["e"], m * P, ops[b]["v"], 0, H)
+            nc.scalar.activation(
+                out=soft[b]["out"][:, m, :],
+                in_=bank[:],
+                func=ACT.Copy,
+                scale=soft[b]["inv_sum"][:, m : m + 1],
+            )
+            nc.sync.dma_start(out=out[b, m * P : (m + 1) * P, :], in_=soft[b]["out"][:, m, :])
+
+        inputs, ops, soft, v_banks, a_banks = {}, {}, {}, {}, {}
+
+        w_raw = load(const, Wv, "w_raw")
+        load_entry(0)
+        bias = const.tile([P, H], BF16, name="bias")
+        nc.sync.dma_start(out=bias[:], in_=bv.partition_broadcast(P))
+        for b in range(1, LOADS_AHEAD - 1):
+            load_entry(b)
+
+        identity = const.tile([P, P], F32, name="identity")
+        make_identity(nc, identity[:])
+        own_mask = const.tile([P, (2 * TILES - 1) * P], F32, name="own_mask")
+        nc.vector.memset(own_mask[:], -MASK_VALUE)
+        nc.gpsimd.affine_select(
+            out=own_mask[:, (TILES - 1) * P : TILES * P],
+            in_=own_mask[:, (TILES - 1) * P : TILES * P],
+            compare_op=ALU.not_equal,
+            fill=MASK_VALUE,
+            base=0,
+            pattern=[[-1, P]],
+            channel_multiplier=1,
+        )
+
+        w_op = mx_operand(const, "w")
+        flip_half(w_raw, w_op, 0)
+        flip_half(w_raw, w_op, 1)
+        quantise(w_op, 0, H)
+
+        for b in range(-1, B):
+            n = b + 1
+            now = b >= 0
+            then = n < B
+            if b + LOADS_AHEAD < B:
+                load_entry(b + LOADS_AHEAD)
+            if then:
+                ops[n] = {name: mx_operand(work, name) for name in ("x", "k", "q", "v", "e")}
+                soft[n] = {
+                    "a": work.tile([P, TILES, L], F32, name="a_sb", tag="a_sb"),
+                    "e": work.tile([P, TILES * L], BF16, name="e_sb", tag="e_sb"),
+                    "neg_max": work.tile([P, TILES], F32, name="neg_max", tag="neg_max"),
+                    "row_sum": work.tile([P, TILES], F32, name="row_sum", tag="row_sum"),
+                    "inv_sum": work.tile([P, TILES], F32, name="inv_sum", tag="inv_sum"),
+                    "out": results.tile([P, TILES, H], F32, name="out_sb", tag="out_sb"),
+                }
+                flip_half(inputs[n]["x"], ops[n]["x"], 0)
+                flip_half(inputs[n]["x"], ops[n]["x"], 1)
+            if now:
+                replace_diagonal(b, 0)
+                replace_diagonal(b, 1)
+                row_maximum(b, 0)
+                exponential(b, 0)
+            if then:
+                flip_half(inputs[n]["k"], ops[n]["k"], 0)
+            if now:
+                replace_diagonal(b, 2)
+                row_maximum(b, 1)
+                exponential(b, 1)
+            if then:
+                quantise(ops[n]["x"], 0, L)
+                flip_half(inputs[n]["k"], ops[n]["k"], 1)
+                project(n)
+            if now:
+                replace_diagonal(b, 3)
+                row_maximum(b, 2)
+                exponential(b, 2)
+                flip_half(soft[b]["e"], ops[b]["e"], 0)
+                row_maximum(b, 3)
+                exponential(b, 3)
+            if then:
+                flip_half(inputs[n]["q"], ops[n]["q"], 0)
+                add_bias(n, 0)
+            if now:
+                quantise(ops[b]["e"], 0, L // 2)
+                flip_half(soft[b]["e"], ops[b]["e"], 1)
+            if then:
+                flip_half(inputs[n]["q"], ops[n]["q"], 1)
+                add_bias(n, 1)
+                add_bias(n, 2)
+            if now:
+                quantise(ops[b]["e"], L // 2, L // 2)
+                nc.vector.reciprocal(out=soft[b]["inv_sum"][:], in_=soft[b]["row_sum"][:])
+            if then:
+                add_bias(n, 3)
+            if now:
+                for m in range(TILES):
+                    mix(b, m)
+            if then:
+                quantise(ops[n]["k"], 0, L)
+                quantise(ops[n]["q"], 0, L)
+                scores(n)
+                quantise(ops[n]["v"], 0, H)

@@ -15,9 +15,10 @@ P = 128
 PACK = 4
 B, L, H = 8, 512, 512
 TILES = L // P
-WORDS = H // 2
+BANK = 512
+PSUM_BANKS = 8
 MASK_VALUE = -3.4028234663852886e38
-LOADS_AHEAD = 4
+LOADS_AHEAD = 3
 
 FLOPS = 3 * 2 * B * L * H * H
 
@@ -26,12 +27,19 @@ def tile_scaleddotproductattention_pa_t_kernel(tc, q, k, x, Wv, bv, out):
     nc = tc.nc
     with ExitStack() as ctx:
         const = ctx.enter_context(tc.tile_pool(name="const", bufs=1))
-        raw = ctx.enter_context(tc.tile_pool(name="raw", bufs=LOADS_AHEAD))
+        raw = ctx.enter_context(tc.tile_pool(name="raw", bufs=LOADS_AHEAD + 1))
         work = ctx.enter_context(tc.tile_pool(name="work", bufs=2))
         results = ctx.enter_context(tc.tile_pool(name="results", bufs=3))
-        flip_banks = ctx.enter_context(tc.psum_pool(name="flip_banks", bufs=3))
-        prod_banks = ctx.enter_context(tc.psum_pool(name="prod_banks", bufs=5))
+        banks = ctx.enter_context(tc.psum_pool(name="banks", bufs=PSUM_BANKS))
         ctx.enter_context(tc.manual_schedule())
+
+        inputs = {}
+        operands = {}
+        soft = {}
+        filled = {}
+
+        def new_bank():
+            return banks.tile([P, BANK], F32, name="bank", tag="bank")
 
         def load(pool, rows, name):
             tile = pool.tile([P, TILES * H], BF16, name=name, tag=name)
@@ -49,12 +57,12 @@ def tile_scaleddotproductattention_pa_t_kernel(tc, q, k, x, Wv, bv, out):
             )
             return tile
 
-        def load_entry(b):
-            inputs[b] = {
-                "x": load_paired(raw, x[b, :, :], "x_raw"),
-                "k": load(raw, k[b, :, :], "k_raw"),
-                "q": load(raw, q[b, :, :], "q_raw"),
-            }
+        def load_scores_inputs(b):
+            inputs["k", b] = load(raw, k[b, :, :], "k_raw")
+            inputs["q", b] = load(raw, q[b, :, :], "q_raw")
+
+        def load_value_input(b):
+            inputs["x", b] = load_paired(raw, x[b, :, :], "x_raw")
 
         def mx_operand(pool, name):
             return {
@@ -63,21 +71,23 @@ def tile_scaleddotproductattention_pa_t_kernel(tc, q, k, x, Wv, bv, out):
                 "scales": pool.tile([P, L], U8, name=name + "_scales", tag=name + "_scales", align_bytes=64),
             }
 
-        def flip_half(source, operand, half):
+        def flip(source, operand):
             words = source[:].bitcast(F32).rearrange("p (s w) -> p s w", s=TILES)
-            bank = flip_banks.tile([P, 2, 2 * P], F32, name="flipped", tag="flipped")
-            for s in range(2):
-                for u in range(2):
-                    nc.tensor.transpose(
-                        bank[:, u, s * P : (s + 1) * P],
-                        words[:, 2 * half + s, u * P : (u + 1) * P],
-                        identity[:],
-                    )
             pairs = operand["grouped"][:].bitcast(F32).rearrange("p (c u) -> p c u", u=2)
-            nc.scalar.copy(
-                out=pairs[:, half * 2 * P : (half + 1) * 2 * P, :],
-                in_=bank[:].rearrange("p u c -> p c u"),
-            )
+            for half in range(2):
+                bank = new_bank()
+                planes = bank[:].rearrange("p (u c) -> p u c", u=2)
+                for s in range(2):
+                    for u in range(2):
+                        nc.tensor.transpose(
+                            planes[:, u, s * P : (s + 1) * P],
+                            words[:, 2 * half + s, u * P : (u + 1) * P],
+                            identity[:],
+                        )
+                nc.scalar.copy(
+                    out=pairs[:, half * 2 * P : (half + 1) * 2 * P, :],
+                    in_=planes.rearrange("p u c -> p c u"),
+                )
 
         def quantise(operand, first, count):
             cols = slice(first, first + count)
@@ -100,79 +110,86 @@ def tile_scaleddotproductattention_pa_t_kernel(tc, q, k, x, Wv, bv, out):
                 stop=True,
             )
 
-        def project(b):
-            v_banks[b] = []
-            for c in range(TILES):
-                bank = prod_banks.tile([P, TILES, P], F32, name="v_bank", tag="product")
-                for t in range(TILES):
-                    mx_pass(bank[:, t, :], ops[b]["x"], t * P, w_op, c * P, P)
-                v_banks[b].append(bank)
+        def flip_scores_inputs(b):
+            for name in ("k", "q"):
+                operands[name, b] = mx_operand(work, name)
+                flip(inputs[name, b], operands[name, b])
 
-        def add_bias(b, c):
-            feats = slice(c * P, (c + 1) * P)
-            grouped = ops[b]["v"]["grouped"][:].rearrange("p (h t) -> p h t", t=PACK)
-            nc.vector.tensor_tensor(
-                out=grouped[:, feats, :],
-                in0=v_banks[b][c][:].rearrange("p t h -> p h t"),
-                in1=bias[:, feats].unsqueeze(2).to_broadcast([P, P, PACK]),
-                op=ALU.add,
-            )
+        def quantise_scores_inputs(b):
+            for name in ("k", "q"):
+                quantise(operands[name, b], 0, L)
 
-        def scores(b):
-            a_banks[b] = []
-            for m in range(TILES):
-                bank = prod_banks.tile([P, L], F32, name="a_bank", tag="product")
-                mx_pass(bank[:], ops[b]["q"], m * P, ops[b]["k"], 0, L)
-                a_banks[b].append(bank)
+        def multiply_scores(b, m):
+            filled["a", b, m] = new_bank()
+            mx_pass(filled["a", b, m][:], operands["q", b], m * P, operands["k", b], 0, L)
 
         def replace_diagonal(b, m):
             nc.vector.tensor_tensor(
-                out=soft[b]["a"][:, m, :],
-                in0=a_banks[b][m][:],
+                out=soft["a", b][:, m, :],
+                in0=filled["a", b, m][:],
                 in1=own_mask[:, (TILES - 1 - m) * P : (TILES - 1 - m) * P + L],
                 op=ALU.min,
             )
 
         def row_maximum(b, m):
             nc.vector.tensor_scalar(
-                out=soft[b]["a"][:, m, :],
-                in0=soft[b]["a"][:, m, :],
+                out=soft["a", b][:, m, :],
+                in0=soft["a", b][:, m, :],
                 scalar1=-1.0 / H,
                 scalar2=None,
                 op0=ALU.mult,
                 op1=ALU.min,
-                accum_out=soft[b]["neg_max"][:, m : m + 1],
+                accum_out=soft["neg_max", b][:, m : m + 1],
             )
 
         def exponential(b, m):
             nc.scalar.activation(
-                out=soft[b]["e"][:, m * L : (m + 1) * L],
-                in_=soft[b]["a"][:, m, :],
+                out=soft["e", b][:, m * L : (m + 1) * L],
+                in_=soft["a", b][:, m, :],
                 func=ACT.Exp,
-                bias=soft[b]["neg_max"][:, m : m + 1],
+                bias=soft["neg_max", b][:, m : m + 1],
                 scale=-1.0,
-                accum_out=soft[b]["row_sum"][:, m : m + 1],
+                accum_out=soft["row_sum", b][:, m : m + 1],
             )
 
-        def mix(b, m):
-            bank = prod_banks.tile([P, H], F32, name="o_bank", tag="product")
-            mx_pass(bank[:], ops[b]["e"], m * P, ops[b]["v"], 0, H)
+        def multiply_values(b):
+            for c in range(TILES):
+                filled["v", b, c] = new_bank()
+                tiles = filled["v", b, c][:].rearrange("p (t h) -> p t h", t=TILES)
+                for t in range(TILES):
+                    mx_pass(tiles[:, t, :], operands["x", b], t * P, w_op, c * P, P)
+
+        def add_bias(b, c):
+            feats = slice(c * P, (c + 1) * P)
+            grouped = operands["v", b]["grouped"][:].rearrange("p (h t) -> p h t", t=PACK)
+            nc.vector.tensor_tensor(
+                out=grouped[:, feats, :],
+                in0=filled["v", b, c][:].rearrange("p (t h) -> p h t", t=TILES),
+                in1=bias[:, feats].unsqueeze(2).to_broadcast([P, P, PACK]),
+                op=ALU.add,
+            )
+
+        def multiply_output(b, m):
+            filled["o", b, m] = new_bank()
+            mx_pass(filled["o", b, m][:], operands["e", b], m * P, operands["v", b], 0, H)
+
+        def divide_and_store(b, m):
             nc.scalar.activation(
-                out=soft[b]["out"][:, m, :],
-                in_=bank[:],
+                out=soft["out", b][:, m, :],
+                in_=filled["o", b, m][:],
                 func=ACT.Copy,
-                scale=soft[b]["inv_sum"][:, m : m + 1],
+                scale=soft["inv_sum", b][:, m : m + 1],
             )
-            nc.sync.dma_start(out=out[b, m * P : (m + 1) * P, :], in_=soft[b]["out"][:, m, :])
+            nc.sync.dma_start(out=out[b, m * P : (m + 1) * P, :], in_=soft["out", b][:, m, :])
 
-        inputs, ops, soft, v_banks, a_banks = {}, {}, {}, {}, {}
-
+        load_scores_inputs(0)
         w_raw = load(const, Wv, "w_raw")
-        load_entry(0)
+        load_value_input(0)
         bias = const.tile([P, H], BF16, name="bias")
         nc.sync.dma_start(out=bias[:], in_=bv.partition_broadcast(P))
-        for b in range(1, LOADS_AHEAD - 1):
-            load_entry(b)
+        for b in range(1, LOADS_AHEAD):
+            load_scores_inputs(b)
+            load_value_input(b)
 
         identity = const.tile([P, P], F32, name="identity")
         make_identity(nc, identity[:])
@@ -187,72 +204,76 @@ def tile_scaleddotproductattention_pa_t_kernel(tc, q, k, x, Wv, bv, out):
             pattern=[[-1, P]],
             channel_multiplier=1,
         )
+        zero = const.tile([P, 1], F32, name="zero")
+        one = const.tile([P, 1], F32, name="one")
+        nc.vector.memset(zero[:], 0.0)
+        nc.scalar.activation(out=one[:], in_=zero[:], func=ACT.Exp)
 
         w_op = mx_operand(const, "w")
-        flip_half(w_raw, w_op, 0)
-        flip_half(w_raw, w_op, 1)
+        flip_scores_inputs(0)
+        flip(w_raw, w_op)
+        quantise_scores_inputs(0)
+        for m in range(TILES):
+            multiply_scores(0, m)
         quantise(w_op, 0, H)
 
-        for b in range(-1, B):
-            n = b + 1
-            now = b >= 0
-            then = n < B
-            if b + LOADS_AHEAD < B:
-                load_entry(b + LOADS_AHEAD)
-            if then:
-                ops[n] = {name: mx_operand(work, name) for name in ("x", "k", "q", "v", "e")}
-                soft[n] = {
-                    "a": work.tile([P, TILES, L], F32, name="a_sb", tag="a_sb"),
-                    "e": work.tile([P, TILES * L], BF16, name="e_sb", tag="e_sb"),
-                    "neg_max": work.tile([P, TILES], F32, name="neg_max", tag="neg_max"),
-                    "row_sum": work.tile([P, TILES], F32, name="row_sum", tag="row_sum"),
-                    "inv_sum": work.tile([P, TILES], F32, name="inv_sum", tag="inv_sum"),
-                    "out": results.tile([P, TILES, H], F32, name="out_sb", tag="out_sb"),
-                }
-                flip_half(inputs[n]["x"], ops[n]["x"], 0)
-                flip_half(inputs[n]["x"], ops[n]["x"], 1)
-            if now:
-                replace_diagonal(b, 0)
-                replace_diagonal(b, 1)
-                row_maximum(b, 0)
-                exponential(b, 0)
-            if then:
-                flip_half(inputs[n]["k"], ops[n]["k"], 0)
-            if now:
-                replace_diagonal(b, 2)
-                row_maximum(b, 1)
-                exponential(b, 1)
-            if then:
-                quantise(ops[n]["x"], 0, L)
-                flip_half(inputs[n]["k"], ops[n]["k"], 1)
-                project(n)
-            if now:
-                replace_diagonal(b, 3)
-                row_maximum(b, 2)
-                exponential(b, 2)
-                flip_half(soft[b]["e"], ops[b]["e"], 0)
-                row_maximum(b, 3)
-                exponential(b, 3)
-            if then:
-                flip_half(inputs[n]["q"], ops[n]["q"], 0)
-                add_bias(n, 0)
-            if now:
-                quantise(ops[b]["e"], 0, L // 2)
-                flip_half(soft[b]["e"], ops[b]["e"], 1)
-            if then:
-                flip_half(inputs[n]["q"], ops[n]["q"], 1)
-                add_bias(n, 1)
-                add_bias(n, 2)
-            if now:
-                quantise(ops[b]["e"], L // 2, L // 2)
-                nc.vector.reciprocal(out=soft[b]["inv_sum"][:], in_=soft[b]["row_sum"][:])
-            if then:
-                add_bias(n, 3)
-            if now:
+        for r in range(B + 1):
+            nxt, cur, prv = r + 1, r, r - 1
+            prepare, soften, finish = nxt < B, cur < B, prv >= 0
+
+            if r + LOADS_AHEAD < B:
+                load_scores_inputs(r + LOADS_AHEAD)
+                load_value_input(r + LOADS_AHEAD)
+
+            if soften:
+                soft["a", cur] = work.tile([P, TILES, L], F32, name="a_sb", tag="a_sb")
+                soft["neg_max", cur] = work.tile([P, TILES], F32, name="neg_max", tag="neg_max")
+                replace_diagonal(cur, 0)
+                replace_diagonal(cur, 1)
+                row_maximum(cur, 0)
+            if finish:
+                quantise(operands["v", prv], 0, H)
+            if soften:
+                operands["x", cur] = mx_operand(work, "x")
+                flip(inputs["x", cur], operands["x", cur])
+                replace_diagonal(cur, 2)
+                row_maximum(cur, 1)
+                replace_diagonal(cur, 3)
+                row_maximum(cur, 2)
+                row_maximum(cur, 3)
+            if finish:
+                operands["e", prv] = mx_operand(work, "e")
+                flip(soft["e", prv], operands["e", prv])
+            if prepare:
+                flip_scores_inputs(nxt)
+
+            if soften:
+                quantise(operands["x", cur], 0, L)
+            if finish:
+                quantise(operands["e", prv], 0, L // 2)
+                quantise(operands["e", prv], L // 2, L // 2)
+                soft["inv_sum", prv] = work.tile([P, TILES], F32, name="inv_sum", tag="inv_sum")
+                nc.vector.reciprocal(out=soft["inv_sum", prv][:], in_=soft["row_sum", prv][:])
+            if prepare:
+                quantise_scores_inputs(nxt)
+
+            if soften:
+                multiply_values(cur)
+            if finish:
                 for m in range(TILES):
-                    mix(b, m)
-            if then:
-                quantise(ops[n]["k"], 0, L)
-                quantise(ops[n]["q"], 0, L)
-                scores(n)
-                quantise(ops[n]["v"], 0, H)
+                    multiply_output(prv, m)
+            if soften:
+                soft["e", cur] = work.tile([P, TILES * L], BF16, name="e_sb", tag="e_sb")
+                soft["row_sum", cur] = work.tile([P, TILES], F32, name="row_sum", tag="row_sum")
+                for m in range(TILES):
+                    exponential(cur, m)
+                operands["v", cur] = mx_operand(work, "v")
+            if finish:
+                soft["out", prv] = results.tile([P, TILES, H], F32, name="out_sb", tag="out_sb")
+            for i in range(TILES):
+                if soften:
+                    add_bias(cur, i)
+                if prepare:
+                    multiply_scores(nxt, i)
+                if finish:
+                    divide_and_store(prv, i)

@@ -23,6 +23,19 @@ LOADS_AHEAD = 3
 FLOPS = 3 * 2 * B * L * H * H
 
 
+def sides(m):
+    return [(first, last) for first, last in ((0, m * P), ((m + 1) * P, L)) if first < last]
+
+
+def passes(first, last):
+    cuts = []
+    while first < last:
+        count = min(2 * P, last - first)
+        cuts.append((first, count))
+        first += count
+    return cuts
+
+
 def tile_scaleddotproductattention_pa_t_kernel(tc, q, k, x, Wv, bv, out):
     nc = tc.nc
     with ExitStack() as ctx:
@@ -119,35 +132,70 @@ def tile_scaleddotproductattention_pa_t_kernel(tc, q, k, x, Wv, bv, out):
             for name in ("k", "q"):
                 quantise(operands[name, b], 0, L)
 
-        def multiply_scores(b, m):
-            filled["a", b, m] = new_bank()
-            mx_pass(filled["a", b, m][:], operands["q", b], m * P, operands["k", b], 0, L)
+        def multiply_scores(b):
+            filled["own", b] = new_bank()
+            blocks = filled["own", b][:].rearrange("p (m c) -> p m c", m=TILES)
+            for m in range(TILES):
+                mx_pass(blocks[:, m, :], operands["q", b], m * P, operands["k", b], m * P, P)
+            for m in range(TILES):
+                filled["others", b, m] = new_bank()
+                for first, last in sides(m):
+                    for start, count in passes(first, last):
+                        mx_pass(
+                            filled["others", b, m][:, start : start + count],
+                            operands["q", b],
+                            m * P,
+                            operands["k", b],
+                            start,
+                            count,
+                        )
 
-        def replace_diagonal(b, m):
-            nc.vector.tensor_tensor(
-                out=soft["a", b][:, m, :],
-                in0=filled["a", b, m][:],
-                in1=own_mask[:, (TILES - 1 - m) * P : (TILES - 1 - m) * P + L],
+        def score_rows(b):
+            return soft["a", b][:, 0 : TILES * L].rearrange("p (m c) -> p m c", c=L)
+
+        def own_blocks(b):
+            return soft["a", b][:].rearrange("p (m c) -> p m c", c=L + P)[:, :, 0:P]
+
+        def replace_diagonal(b):
+            nc.vector.scalar_tensor_tensor(
+                out=own_blocks(b),
+                in0=filled["own", b][:].rearrange("p (m c) -> p m c", m=TILES),
+                scalar=-1.0 / H,
+                in1=own_mask[:].unsqueeze(1).to_broadcast([P, TILES, P]),
+                op0=ALU.mult,
+                op1=ALU.max,
+            )
+
+        def own_minimum(b):
+            nc.vector.tensor_reduce(
+                out=soft["own_min", b][:],
+                in_=own_blocks(b),
+                axis=mybir.AxisListType.X,
                 op=ALU.min,
             )
 
-        def row_maximum(b, m):
-            nc.vector.tensor_scalar(
-                out=soft["a", b][:, m, :],
-                in0=soft["a", b][:, m, :],
-                scalar1=-1.0 / H,
-                scalar2=None,
-                op0=ALU.mult,
-                op1=ALU.min,
-                accum_out=soft["neg_max", b][:, m : m + 1],
-            )
+        def take_others(b, m):
+            running = soft["own_min", b][:, m : m + 1]
+            for side, (first, last) in enumerate(sides(m)):
+                carried = soft["run_min", b][:, m, side : side + 1]
+                nc.vector.tensor_scalar(
+                    out=score_rows(b)[:, m, first:last],
+                    in0=filled["others", b, m][:, first:last],
+                    scalar1=-1.0 / H,
+                    scalar2=running,
+                    op0=ALU.mult,
+                    op1=ALU.min,
+                    accum_out=carried,
+                )
+                running = carried
+            soft["neg_max", b, m] = running
 
         def exponential(b, m):
             nc.scalar.activation(
                 out=soft["e", b][:, m * L : (m + 1) * L],
-                in_=soft["a", b][:, m, :],
+                in_=score_rows(b)[:, m, :],
                 func=ACT.Exp,
-                bias=soft["neg_max", b][:, m : m + 1],
+                bias=soft["neg_max", b, m],
                 scale=-1.0,
                 accum_out=soft["row_sum", b][:, m : m + 1],
             )
@@ -193,13 +241,13 @@ def tile_scaleddotproductattention_pa_t_kernel(tc, q, k, x, Wv, bv, out):
 
         identity = const.tile([P, P], F32, name="identity")
         make_identity(nc, identity[:])
-        own_mask = const.tile([P, (2 * TILES - 1) * P], F32, name="own_mask")
-        nc.vector.memset(own_mask[:], -MASK_VALUE)
+        own_mask = const.tile([P, P], F32, name="own_mask")
+        nc.vector.memset(own_mask[:], MASK_VALUE)
         nc.gpsimd.affine_select(
-            out=own_mask[:, (TILES - 1) * P : TILES * P],
-            in_=own_mask[:, (TILES - 1) * P : TILES * P],
+            out=own_mask[:],
+            in_=own_mask[:],
             compare_op=ALU.not_equal,
-            fill=MASK_VALUE,
+            fill=-MASK_VALUE,
             base=0,
             pattern=[[-1, P]],
             channel_multiplier=1,
@@ -213,8 +261,7 @@ def tile_scaleddotproductattention_pa_t_kernel(tc, q, k, x, Wv, bv, out):
         flip_scores_inputs(0)
         flip(w_raw, w_op)
         quantise_scores_inputs(0)
-        for m in range(TILES):
-            multiply_scores(0, m)
+        multiply_scores(0)
         quantise(w_op, 0, H)
 
         for r in range(B + 1):
@@ -226,24 +273,22 @@ def tile_scaleddotproductattention_pa_t_kernel(tc, q, k, x, Wv, bv, out):
                 load_value_input(r + LOADS_AHEAD)
 
             if soften:
-                soft["a", cur] = work.tile([P, TILES, L], F32, name="a_sb", tag="a_sb")
-                soft["neg_max", cur] = work.tile([P, TILES], F32, name="neg_max", tag="neg_max")
-                replace_diagonal(cur, 0)
-                replace_diagonal(cur, 1)
-                row_maximum(cur, 0)
+                soft["a", cur] = work.tile([P, (TILES + 1) * L], F32, name="a_sb", tag="a_sb")
+                soft["own_min", cur] = work.tile([P, TILES], F32, name="own_min", tag="own_min")
+                soft["run_min", cur] = work.tile([P, TILES, 2], F32, name="run_min", tag="run_min")
+                replace_diagonal(cur)
             if finish:
                 quantise(operands["v", prv], 0, H)
             if soften:
+                own_minimum(cur)
                 operands["x", cur] = mx_operand(work, "x")
                 flip(inputs["x", cur], operands["x", cur])
-                replace_diagonal(cur, 2)
-                row_maximum(cur, 1)
-                replace_diagonal(cur, 3)
-                row_maximum(cur, 2)
-                row_maximum(cur, 3)
             if finish:
                 operands["e", prv] = mx_operand(work, "e")
                 flip(soft["e", prv], operands["e", prv])
+            if soften:
+                for m in range(TILES):
+                    take_others(cur, m)
             if prepare:
                 flip_scores_inputs(nxt)
 
@@ -270,10 +315,13 @@ def tile_scaleddotproductattention_pa_t_kernel(tc, q, k, x, Wv, bv, out):
                 operands["v", cur] = mx_operand(work, "v")
             if finish:
                 soft["out", prv] = results.tile([P, TILES, H], F32, name="out_sb", tag="out_sb")
-            for i in range(TILES):
-                if soften:
-                    add_bias(cur, i)
-                if prepare:
-                    multiply_scores(nxt, i)
-                if finish:
-                    divide_and_store(prv, i)
+            if soften:
+                for c in range(TILES):
+                    add_bias(cur, c)
+            if finish:
+                divide_and_store(prv, 0)
+            if prepare:
+                multiply_scores(nxt)
+            if finish:
+                for m in range(1, TILES):
+                    divide_and_store(prv, m)

@@ -19,6 +19,7 @@ BANK = 512
 PSUM_BANKS = 8
 MASK_VALUE = -3.4028234663852886e38
 LOADS_AHEAD = 3
+SCALAR_DIVIDES = 3
 
 FLOPS = 3 * 2 * B * L * H * H
 
@@ -222,12 +223,21 @@ def tile_scaleddotproductattention_pa_t_kernel(tc, q, k, x, Wv, bv, out):
             mx_pass(filled["o", b, m][:], operands["e", b], m * P, operands["v", b], 0, H)
 
         def divide_and_store(b, m):
-            nc.scalar.activation(
-                out=soft["out", b][:, m, :],
-                in_=filled["o", b, m][:],
-                func=ACT.Copy,
-                scale=soft["inv_sum", b][:, m : m + 1],
-            )
+            if m < SCALAR_DIVIDES:
+                nc.scalar.activation(
+                    out=soft["out", b][:, m, :],
+                    in_=filled["o", b, m][:],
+                    func=ACT.Copy,
+                    scale=soft["inv_sum", b][:, m : m + 1],
+                )
+            else:
+                nc.vector.tensor_scalar(
+                    out=soft["out", b][:, m, :],
+                    in0=filled["o", b, m][:],
+                    scalar1=soft["inv_sum", b][:, m : m + 1],
+                    scalar2=None,
+                    op0=ALU.mult,
+                )
             nc.sync.dma_start(out=out[b, m * P : (m + 1) * P, :], in_=soft["out", b][:, m, :])
 
         load_scores_inputs(0)

@@ -19,7 +19,6 @@ BANK = 512
 PSUM_BANKS = 8
 MASK_VALUE = -3.4028234663852886e38
 LOADS_AHEAD = 3
-SCALAR_DIVIDES = 3
 
 FLOPS = 3 * 2 * B * L * H * H
 
@@ -124,32 +123,28 @@ def tile_scaleddotproductattention_pa_t_kernel(tc, q, k, x, Wv, bv, out):
                 stop=True,
             )
 
-        def flip_scores_inputs(b):
-            for name in ("k", "q"):
-                operands[name, b] = mx_operand(work, name)
-                flip(inputs[name, b], operands[name, b])
+        def flip_input(name, b):
+            operands[name, b] = mx_operand(work, name)
+            flip(inputs[name, b], operands[name, b])
 
-        def quantise_scores_inputs(b):
-            for name in ("k", "q"):
-                quantise(operands[name, b], 0, L)
-
-        def multiply_scores(b):
+        def multiply_own_scores(b):
             filled["own", b] = new_bank()
             blocks = filled["own", b][:].rearrange("p (m c) -> p m c", m=TILES)
             for m in range(TILES):
                 mx_pass(blocks[:, m, :], operands["q", b], m * P, operands["k", b], m * P, P)
-            for m in range(TILES):
-                filled["others", b, m] = new_bank()
-                for first, last in sides(m):
-                    for start, count in passes(first, last):
-                        mx_pass(
-                            filled["others", b, m][:, start : start + count],
-                            operands["q", b],
-                            m * P,
-                            operands["k", b],
-                            start,
-                            count,
-                        )
+
+        def multiply_other_scores(b, m):
+            filled["others", b, m] = new_bank()
+            for first, last in sides(m):
+                for start, count in passes(first, last):
+                    mx_pass(
+                        filled["others", b, m][:, start : start + count],
+                        operands["q", b],
+                        m * P,
+                        operands["k", b],
+                        start,
+                        count,
+                    )
 
         def score_rows(b):
             return soft["a", b][:, 0 : TILES * L].rearrange("p (m c) -> p m c", c=L)
@@ -201,12 +196,11 @@ def tile_scaleddotproductattention_pa_t_kernel(tc, q, k, x, Wv, bv, out):
                 accum_out=soft["row_sum", b][:, m : m + 1],
             )
 
-        def multiply_values(b):
-            for c in range(TILES):
-                filled["v", b, c] = new_bank()
-                tiles = filled["v", b, c][:].rearrange("p (t h) -> p t h", t=TILES)
-                for t in range(TILES):
-                    mx_pass(tiles[:, t, :], operands["x", b], t * P, w_op, c * P, P)
+        def multiply_values(b, c):
+            filled["v", b, c] = new_bank()
+            tiles = filled["v", b, c][:].rearrange("p (t h) -> p t h", t=TILES)
+            for t in range(TILES):
+                mx_pass(tiles[:, t, :], operands["x", b], t * P, w_op, c * P, P)
 
         def add_bias(b, c):
             feats = slice(c * P, (c + 1) * P)
@@ -223,21 +217,12 @@ def tile_scaleddotproductattention_pa_t_kernel(tc, q, k, x, Wv, bv, out):
             mx_pass(filled["o", b, m][:], operands["e", b], m * P, operands["v", b], 0, H)
 
         def divide_and_store(b, m):
-            if m < SCALAR_DIVIDES:
-                nc.scalar.activation(
-                    out=soft["out", b][:, m, :],
-                    in_=filled["o", b, m][:],
-                    func=ACT.Copy,
-                    scale=soft["inv_sum", b][:, m : m + 1],
-                )
-            else:
-                nc.vector.tensor_scalar(
-                    out=soft["out", b][:, m, :],
-                    in0=filled["o", b, m][:],
-                    scalar1=soft["inv_sum", b][:, m : m + 1],
-                    scalar2=None,
-                    op0=ALU.mult,
-                )
+            nc.scalar.activation(
+                out=soft["out", b][:, m, :],
+                in_=filled["o", b, m][:],
+                func=ACT.Copy,
+                scale=soft["inv_sum", b][:, m : m + 1],
+            )
             nc.sync.dma_start(out=out[b, m * P : (m + 1) * P, :], in_=soft["out", b][:, m, :])
 
         load_scores_inputs(0)
@@ -268,10 +253,13 @@ def tile_scaleddotproductattention_pa_t_kernel(tc, q, k, x, Wv, bv, out):
         nc.scalar.activation(out=one[:], in_=zero[:], func=ACT.Exp)
 
         w_op = mx_operand(const, "w")
-        flip_scores_inputs(0)
+        flip_input("k", 0)
+        flip_input("q", 0)
         flip(w_raw, w_op)
-        quantise_scores_inputs(0)
-        multiply_scores(0)
+        flip_input("x", 0)
+        quantise(operands["k", 0], 0, L)
+        quantise(operands["q", 0], 0, L)
+        multiply_own_scores(0)
         quantise(w_op, 0, H)
 
         for r in range(B + 1):
@@ -289,49 +277,56 @@ def tile_scaleddotproductattention_pa_t_kernel(tc, q, k, x, Wv, bv, out):
                 replace_diagonal(cur)
             if finish:
                 quantise(operands["v", prv], 0, H)
-            if soften:
-                own_minimum(cur)
-                operands["x", cur] = mx_operand(work, "x")
-                flip(inputs["x", cur], operands["x", cur])
-            if finish:
                 operands["e", prv] = mx_operand(work, "e")
                 flip(soft["e", prv], operands["e", prv])
-            if soften:
-                for m in range(TILES):
-                    take_others(cur, m)
             if prepare:
-                flip_scores_inputs(nxt)
-
+                flip_input("k", nxt)
             if soften:
-                quantise(operands["x", cur], 0, L)
+                own_minimum(cur)
             if finish:
                 quantise(operands["e", prv], 0, L // 2)
                 quantise(operands["e", prv], L // 2, L // 2)
                 soft["inv_sum", prv] = work.tile([P, TILES], F32, name="inv_sum", tag="inv_sum")
                 nc.vector.reciprocal(out=soft["inv_sum", prv][:], in_=soft["row_sum", prv][:])
+            if soften:
+                quantise(operands["x", cur], 0, L)
+                multiply_other_scores(cur, 0)
+                multiply_other_scores(cur, 1)
             if prepare:
-                quantise_scores_inputs(nxt)
-
+                flip_input("q", nxt)
+                flip_input("x", nxt)
             if soften:
-                multiply_values(cur)
-            if finish:
-                for m in range(TILES):
-                    multiply_output(prv, m)
+                take_others(cur, 0)
+                take_others(cur, 1)
+            if prepare:
+                quantise(operands["k", nxt], 0, L)
             if soften:
+                operands["v", cur] = mx_operand(work, "v")
+                multiply_values(cur, 0)
+                multiply_other_scores(cur, 2)
+                multiply_values(cur, 1)
+                multiply_other_scores(cur, 3)
+                multiply_values(cur, 2)
+                multiply_values(cur, 3)
+                add_bias(cur, 0)
+                take_others(cur, 2)
+                take_others(cur, 3)
+                add_bias(cur, 1)
+            if prepare:
+                quantise(operands["q", nxt], 0, L)
+            if soften:
+                add_bias(cur, 2)
+                add_bias(cur, 3)
                 soft["e", cur] = work.tile([P, TILES * L], BF16, name="e_sb", tag="e_sb")
                 soft["row_sum", cur] = work.tile([P, TILES], F32, name="row_sum", tag="row_sum")
                 for m in range(TILES):
                     exponential(cur, m)
-                operands["v", cur] = mx_operand(work, "v")
+            if finish:
+                for m in range(TILES):
+                    multiply_output(prv, m)
+            if prepare:
+                multiply_own_scores(nxt)
             if finish:
                 soft["out", prv] = results.tile([P, TILES, H], F32, name="out_sb", tag="out_sb")
-            if soften:
-                for c in range(TILES):
-                    add_bias(cur, c)
-            if finish:
-                divide_and_store(prv, 0)
-            if prepare:
-                multiply_scores(nxt)
-            if finish:
-                for m in range(1, TILES):
+                for m in range(TILES):
                     divide_and_store(prv, m)

@@ -17,7 +17,7 @@ B, L, H = 8, 512, 512
 TILES = L // P
 BANK = 512
 PSUM_BANKS = 8
-MASK_VALUE = -3.4028234663852886e38
+BIG = 2.0**60
 LOADS_AHEAD = 3
 
 FLOPS = 3 * 2 * B * L * H * H
@@ -84,23 +84,30 @@ def tile_scaleddotproductattention_pa_t_kernel(tc, q, k, x, Wv, bv, out):
                 "scales": pool.tile([P, L], U8, name=name + "_scales", tag=name + "_scales", align_bytes=64),
             }
 
-        def flip(source, operand):
+        def turn(source, key, half):
             words = source[:].bitcast(F32).rearrange("p (s w) -> p s w", s=TILES)
+            filled["t", key, half] = new_bank()
+            planes = filled["t", key, half][:].rearrange("p (u c) -> p u c", u=2)
+            for s in range(2):
+                for u in range(2):
+                    nc.tensor.transpose(
+                        planes[:, u, s * P : (s + 1) * P],
+                        words[:, 2 * half + s, u * P : (u + 1) * P],
+                        identity[:],
+                    )
+
+        def collect(operand, key, half, copy):
             pairs = operand["grouped"][:].bitcast(F32).rearrange("p (c u) -> p c u", u=2)
+            planes = filled["t", key, half][:].rearrange("p (u c) -> p u c", u=2)
+            copy(
+                out=pairs[:, half * 2 * P : (half + 1) * 2 * P, :],
+                in_=planes.rearrange("p u c -> p c u"),
+            )
+
+        def flip(source, operand, key):
             for half in range(2):
-                bank = new_bank()
-                planes = bank[:].rearrange("p (u c) -> p u c", u=2)
-                for s in range(2):
-                    for u in range(2):
-                        nc.tensor.transpose(
-                            planes[:, u, s * P : (s + 1) * P],
-                            words[:, 2 * half + s, u * P : (u + 1) * P],
-                            identity[:],
-                        )
-                nc.scalar.copy(
-                    out=pairs[:, half * 2 * P : (half + 1) * 2 * P, :],
-                    in_=planes.rearrange("p u c -> p c u"),
-                )
+                turn(source, key, half)
+                collect(operand, key, half, nc.scalar.copy)
 
         def quantise(operand, first, count):
             cols = slice(first, first + count)
@@ -110,7 +117,7 @@ def tile_scaleddotproductattention_pa_t_kernel(tc, q, k, x, Wv, bv, out):
                 in_=operand["grouped"][:, first * PACK : (first + count) * PACK],
             )
 
-        def mx_pass(acc, stationary, s_first, moving, m_first, m_count):
+        def mx_pass(acc, stationary, s_first, moving, m_first, m_count, start=True, stop=True):
             s_cols = slice(s_first, s_first + P)
             m_cols = slice(m_first, m_first + m_count)
             nc.tensor.matmul_mx(
@@ -119,79 +126,44 @@ def tile_scaleddotproductattention_pa_t_kernel(tc, q, k, x, Wv, bv, out):
                 lhsT_scale=stationary["scales"][:, s_cols],
                 rhs=moving["codes"][:, m_cols].bitcast(FP8X4),
                 rhs_scale=moving["scales"][:, m_cols],
-                start=True,
-                stop=True,
+                start=start,
+                stop=stop,
             )
 
         def flip_input(name, b):
             operands[name, b] = mx_operand(work, name)
-            flip(inputs[name, b], operands[name, b])
+            flip(inputs[name, b], operands[name, b], (name, b))
 
-        def multiply_own_scores(b):
-            filled["own", b] = new_bank()
-            blocks = filled["own", b][:].rearrange("p (m c) -> p m c", m=TILES)
-            for m in range(TILES):
-                mx_pass(blocks[:, m, :], operands["q", b], m * P, operands["k", b], m * P, P)
-
-        def multiply_other_scores(b, m):
-            filled["others", b, m] = new_bank()
+        def multiply_scores(b, m):
+            filled["s", b, m] = new_bank()
+            bank = filled["s", b, m]
             for first, last in sides(m):
                 for start, count in passes(first, last):
-                    mx_pass(
-                        filled["others", b, m][:, start : start + count],
-                        operands["q", b],
-                        m * P,
-                        operands["k", b],
-                        start,
-                        count,
-                    )
+                    mx_pass(bank[:, start : start + count], operands["q", b], m * P, operands["k", b], start, count)
+            own = bank[:, m * P : (m + 1) * P]
+            mx_pass(own, operands["q", b], m * P, operands["k", b], m * P, P, start=True, stop=False)
+            mx_pass(own, diag, 0, diag, P, P, start=False, stop=True)
 
         def score_rows(b):
-            return soft["a", b][:, 0 : TILES * L].rearrange("p (m c) -> p m c", c=L)
+            return soft["a", b][:].rearrange("p (m c) -> p m c", c=L)
 
-        def own_blocks(b):
-            return soft["a", b][:].rearrange("p (m c) -> p m c", c=L + P)[:, :, 0:P]
-
-        def replace_diagonal(b):
-            nc.vector.scalar_tensor_tensor(
-                out=own_blocks(b),
-                in0=filled["own", b][:].rearrange("p (m c) -> p m c", m=TILES),
-                scalar=-1.0 / H,
-                in1=own_mask[:].unsqueeze(1).to_broadcast([P, TILES, P]),
+        def take_scores(b, m):
+            nc.vector.tensor_scalar(
+                out=score_rows(b)[:, m, :],
+                in0=filled["s", b, m][:],
+                scalar1=-1.0 / H,
+                scalar2=None,
                 op0=ALU.mult,
-                op1=ALU.max,
+                op1=ALU.min,
+                accum_out=soft["neg_max", b][:, m : m + 1],
             )
-
-        def own_minimum(b):
-            nc.vector.tensor_reduce(
-                out=soft["own_min", b][:],
-                in_=own_blocks(b),
-                axis=mybir.AxisListType.X,
-                op=ALU.min,
-            )
-
-        def take_others(b, m):
-            running = soft["own_min", b][:, m : m + 1]
-            for side, (first, last) in enumerate(sides(m)):
-                carried = soft["run_min", b][:, m, side : side + 1]
-                nc.vector.tensor_scalar(
-                    out=score_rows(b)[:, m, first:last],
-                    in0=filled["others", b, m][:, first:last],
-                    scalar1=-1.0 / H,
-                    scalar2=running,
-                    op0=ALU.mult,
-                    op1=ALU.min,
-                    accum_out=carried,
-                )
-                running = carried
-            soft["neg_max", b, m] = running
 
         def exponential(b, m):
             nc.scalar.activation(
                 out=soft["e", b][:, m * L : (m + 1) * L],
                 in_=score_rows(b)[:, m, :],
                 func=ACT.Exp,
-                bias=soft["neg_max", b, m],
+                bias=soft["neg_max", b][:, m : m + 1],
                 scale=-1.0,
                 accum_out=soft["row_sum", b][:, m : m + 1],
             )
@@ -236,17 +208,16 @@ def tile_scaleddotproductattention_pa_t_kernel(tc, q, k, x, Wv, bv, out):
 
         identity = const.tile([P, P], F32, name="identity")
         make_identity(nc, identity[:])
-        own_mask = const.tile([P, P], F32, name="own_mask")
-        nc.vector.memset(own_mask[:], MASK_VALUE)
-        nc.gpsimd.affine_select(
-            out=own_mask[:],
-            in_=own_mask[:],
-            compare_op=ALU.not_equal,
-            fill=-MASK_VALUE,
-            base=0,
-            pattern=[[-1, P]],
-            channel_multiplier=1,
-        )
+        diag = {
+            "grouped": const.tile([P, 2 * P * PACK], BF16, name="diag_grouped", align_bytes=64),
+            "codes": const.tile([P, 2 * P], U32, name="diag_codes", align_bytes=64),
+            "scales": const.tile([P, 2 * P], U8, name="diag_scales", align_bytes=64),
+        }
+        nc.vector.memset(diag["grouped"][:], 0.0)
+        slots = diag["grouped"][:].rearrange("p (s c t) -> p s c t", s=2, t=PACK)
+        nc.vector.tensor_scalar_mul(out=slots[:, 0, :, 0], in0=identity[:], scalar1=-BIG)
+        nc.vector.tensor_scalar_mul(out=slots[:, 1, :, 0], in0=identity[:], scalar1=BIG)
+        quantise(diag, 0, 2 * P)
         zero = const.tile([P, 1], F32, name="zero")
         one = const.tile([P, 1], F32, name="one")
         nc.vector.memset(zero[:], 0.0)
@@ -255,11 +226,11 @@ def tile_scaleddotproductattention_pa_t_kernel(tc, q, k, x, Wv, bv, out):
         w_op = mx_operand(const, "w")
         flip_input("k", 0)
         flip_input("q", 0)
-        flip(w_raw, w_op)
+        flip(w_raw, w_op, "w")
         flip_input("x", 0)
         quantise(operands["k", 0], 0, L)
         quantise(operands["q", 0], 0, L)
-        multiply_own_scores(0)
+        multiply_scores(0, 0)
         quantise(w_op, 0, H)
 
         for r in range(B + 1):
@@ -271,18 +242,15 @@ def tile_scaleddotproductattention_pa_t_kernel(tc, q, k, x, Wv, bv, out):
                 load_value_input(r + LOADS_AHEAD)
 
             if soften:
-                soft["a", cur] = work.tile([P, (TILES + 1) * L], F32, name="a_sb", tag="a_sb")
-                soft["own_min", cur] = work.tile([P, TILES], F32, name="own_min", tag="own_min")
-                soft["run_min", cur] = work.tile([P, TILES, 2], F32, name="run_min", tag="run_min")
-                replace_diagonal(cur)
+                soft["a", cur] = work.tile([P, TILES * L], F32, name="a_sb", tag="a_sb")
+                soft["neg_max", cur] = work.tile([P, TILES], F32, name="neg_max", tag="neg_max")
+                take_scores(cur, 0)
             if finish:
                 quantise(operands["v", prv], 0, H)
                 operands["e", prv] = mx_operand(work, "e")
-                flip(soft["e", prv], operands["e", prv])
+                flip(soft["e", prv], operands["e", prv], ("e", prv))
             if prepare:
                 flip_input("k", nxt)
-            if soften:
-                own_minimum(cur)
             if finish:
                 quantise(operands["e", prv], 0, L // 2)
                 quantise(operands["e", prv], L // 2, L // 2)
@@ -290,27 +258,31 @@ def tile_scaleddotproductattention_pa_t_kernel(tc, q, k, x, Wv, bv, out):
                 nc.vector.reciprocal(out=soft["inv_sum", prv][:], in_=soft["row_sum", prv][:])
             if soften:
                 quantise(operands["x", cur], 0, L)
-                multiply_other_scores(cur, 0)
-                multiply_other_scores(cur, 1)
+                multiply_scores(cur, 1)
             if prepare:
                 flip_input("q", nxt)
-                flip_input("x", nxt)
+                operands["x", nxt] = mx_operand(work, "x")
+                turn(inputs["x", nxt], ("x", nxt), 0)
+                collect(operands["x", nxt], ("x", nxt), 0, nc.scalar.copy)
+                turn(inputs["x", nxt], ("x", nxt), 1)
             if soften:
-                take_others(cur, 0)
-                take_others(cur, 1)
+                take_scores(cur, 1)
             if prepare:
                 quantise(operands["k", nxt], 0, L)
             if soften:
                 operands["v", cur] = mx_operand(work, "v")
                 multiply_values(cur, 0)
-                multiply_other_scores(cur, 2)
+                multiply_scores(cur, 2)
                 multiply_values(cur, 1)
-                multiply_other_scores(cur, 3)
+                multiply_scores(cur, 3)
                 multiply_values(cur, 2)
                 multiply_values(cur, 3)
                 add_bias(cur, 0)
-                take_others(cur, 2)
-                take_others(cur, 3)
+                take_scores(cur, 2)
+                take_scores(cur, 3)
+            if prepare:
+                collect(operands["x", nxt], ("x", nxt), 1, nc.vector.tensor_copy)
+            if soften:
                 add_bias(cur, 1)
             if prepare:
                 quantise(operands["q", nxt], 0, L)
@@ -325,7 +297,7 @@ def tile_scaleddotproductattention_pa_t_kernel(tc, q, k, x, Wv, bv, out):
                 for m in range(TILES):
                     multiply_output(prv, m)
             if prepare:
-                multiply_own_scores(nxt)
+                multiply_scores(nxt, 0)
             if finish:
                 soft["out", prv] = results.tile([P, TILES, H], F32, name="out_sb", tag="out_sb")
                 for m in range(TILES):

@@ -19,6 +19,9 @@ BANK = 512
 PSUM_BANKS = 8
 BIG = 2.0**60
 LOADS_AHEAD = 3
+FIRST_STEP = -TILES
+W_STEP = -2
+LAST_STEP = TILES * (B + 2)
 
 FLOPS = 3 * 2 * B * L * H * H
 
@@ -42,14 +45,18 @@ def tile_scaleddotproductattention_pa_t_kernel(tc, q, k, x, Wv, bv, out):
         const = ctx.enter_context(tc.tile_pool(name="const", bufs=1))
         raw = ctx.enter_context(tc.tile_pool(name="raw", bufs=LOADS_AHEAD + 1))
         work = ctx.enter_context(tc.tile_pool(name="work", bufs=2))
-        results = ctx.enter_context(tc.tile_pool(name="results", bufs=3))
+        results = ctx.enter_context(tc.tile_pool(name="results", bufs=6))
         banks = ctx.enter_context(tc.psum_pool(name="banks", bufs=PSUM_BANKS))
         ctx.enter_context(tc.manual_schedule())
 
         inputs = {}
-        operands = {}
+        grouped = {}
+        coded = {}
         soft = {}
         filled = {}
+
+        def live(b):
+            return 0 <= b < B
 
         def new_bank():
             return banks.tile([P, BANK], F32, name="bank", tag="bank")
@@ -70,22 +77,17 @@ def tile_scaleddotproductattention_pa_t_kernel(tc, q, k, x, Wv, bv, out):
             )
             return tile
 
-        def load_scores_inputs(b):
+        def load_entry(b):
             inputs["k", b] = load(raw, k[b, :, :], "k_raw")
             inputs["q", b] = load(raw, q[b, :, :], "q_raw")
-
-        def load_value_input(b):
             inputs["x", b] = load_paired(raw, x[b, :, :], "x_raw")
 
-        def mx_operand(pool, name):
-            return {
-                "grouped": pool.tile([P, L * PACK], BF16, name=name + "_grouped", tag=name + "_grouped", align_bytes=64),
-                "codes": pool.tile([P, L], U32, name=name + "_codes", tag=name + "_codes", align_bytes=64),
-                "scales": pool.tile([P, L], U8, name=name + "_scales", tag=name + "_scales", align_bytes=64),
-            }
+        def new_grouped(key):
+            name = key[0] + "_grouped"
+            grouped[key] = work.tile([P, L * PACK], BF16, name=name, tag=name, align_bytes=64)
 
-        def turn(source, key, half):
-            words = source[:].bitcast(F32).rearrange("p (s w) -> p s w", s=TILES)
+        def turn(key, half):
+            words = inputs[key][:].bitcast(F32).rearrange("p (s w) -> p s w", s=TILES)
             filled["t", key, half] = new_bank()
             planes = filled["t", key, half][:].rearrange("p (u c) -> p u c", u=2)
             for s in range(2):
@@ -96,60 +98,47 @@ def tile_scaleddotproductattention_pa_t_kernel(tc, q, k, x, Wv, bv, out):
                         identity[:],
                     )
 
-        def collect(operand, key, half, copy):
-            pairs = operand["grouped"][:].bitcast(F32).rearrange("p (c u) -> p c u", u=2)
+        def collect(key, half, copy):
+            pairs = grouped[key][:].bitcast(F32).rearrange("p (c u) -> p c u", u=2)
             planes = filled["t", key, half][:].rearrange("p (u c) -> p u c", u=2)
             copy(
                 out=pairs[:, half * 2 * P : (half + 1) * 2 * P, :],
                 in_=planes.rearrange("p u c -> p c u"),
             )
 
-        def flip(source, operand, key):
-            for half in range(2):
-                turn(source, key, half)
-                collect(operand, key, half, nc.scalar.copy)
-
-        def quantise(operand, first, count):
-            cols = slice(first, first + count)
-            nc.vector.quantize_mx(
-                out=operand["codes"][:, cols].bitcast(FP8X4),
-                scales=operand["scales"][:, cols],
-                in_=operand["grouped"][:, first * PACK : (first + count) * PACK],
-            )
+        def quantise(key):
+            name = key[0]
+            codes = work.tile([P, L], U32, name=name + "_codes", tag=name + "_codes", align_bytes=64)
+            scales = work.tile([P, L], U8, name=name + "_scales", tag=name + "_scales", align_bytes=64)
+            nc.vector.quantize_mx(out=codes[:].bitcast(FP8X4), scales=scales[:], in_=grouped[key][:])
+            coded[key] = (codes, scales)
 
         def mx_pass(acc, stationary, s_first, moving, m_first, m_count, start=True, stop=True):
             s_cols = slice(s_first, s_first + P)
             m_cols = slice(m_first, m_first + m_count)
             nc.tensor.matmul_mx(
                 out=acc,
-                lhsT=stationary["codes"][:, s_cols].bitcast(FP8X4),
-                lhsT_scale=stationary["scales"][:, s_cols],
-                rhs=moving["codes"][:, m_cols].bitcast(FP8X4),
-                rhs_scale=moving["scales"][:, m_cols],
+                lhsT=stationary[0][:, s_cols].bitcast(FP8X4),
+                lhsT_scale=stationary[1][:, s_cols],
+                rhs=moving[0][:, m_cols].bitcast(FP8X4),
+                rhs_scale=moving[1][:, m_cols],
                 start=start,
                 stop=stop,
             )
-
-        def flip_input(name, b):
-            operands[name, b] = mx_operand(work, name)
-            flip(inputs[name, b], operands[name, b], (name, b))
 
         def multiply_scores(b, m):
             filled["s", b, m] = new_bank()
             bank = filled["s", b, m]
             for first, last in sides(m):
                 for start, count in passes(first, last):
-                    mx_pass(bank[:, start : start + count], operands["q", b], m * P, operands["k", b], start, count)
+                    mx_pass(bank[:, start : start + count], coded["q", b], m * P, coded["k", b], start, count)
             own = bank[:, m * P : (m + 1) * P]
-            mx_pass(own, operands["q", b], m * P, operands["k", b], m * P, P, start=True, stop=False)
+            mx_pass(own, coded["q", b], m * P, coded["k", b], m * P, P, start=True, stop=False)
             mx_pass(own, diag, 0, diag, P, P, start=False, stop=True)
-
-        def score_rows(b):
-            return soft["a", b][:].rearrange("p (m c) -> p m c", c=L)
 
         def take_scores(b, m):
             nc.vector.tensor_scalar(
-                out=score_rows(b)[:, m, :],
+                out=soft["a", b][:, m * L : (m + 1) * L],
                 in0=filled["s", b, m][:],
                 scalar1=-1.0 / H,
                 scalar2=None,
@@ -160,8 +149,8 @@ def tile_scaleddotproductattention_pa_t_kernel(tc, q, k, x, Wv, bv, out):
 
         def exponential(b, m):
             nc.scalar.activation(
-                out=soft["e", b][:, m * L : (m + 1) * L],
-                in_=score_rows(b)[:, m, :],
+                out=inputs["e", b][:, m * L : (m + 1) * L],
+                in_=soft["a", b][:, m * L : (m + 1) * L],
                 func=ACT.Exp,
                 bias=soft["neg_max", b][:, m : m + 1],
                 scale=-1.0,
@@ -172,13 +161,12 @@ def tile_scaleddotproductattention_pa_t_kernel(tc, q, k, x, Wv, bv, out):
             filled["v", b, c] = new_bank()
             tiles = filled["v", b, c][:].rearrange("p (t h) -> p t h", t=TILES)
             for t in range(TILES):
-                mx_pass(tiles[:, t, :], operands["x", b], t * P, w_op, c * P, P)
+                mx_pass(tiles[:, t, :], coded["x", b], t * P, coded["w", 0], c * P, P)
 
         def add_bias(b, c):
             feats = slice(c * P, (c + 1) * P)
-            grouped = operands["v", b]["grouped"][:].rearrange("p (h t) -> p h t", t=PACK)
             nc.vector.tensor_tensor(
-                out=grouped[:, feats, :],
+                out=grouped["v", b][:].rearrange("p (h t) -> p h t", t=PACK)[:, feats, :],
                 in0=filled["v", b, c][:].rearrange("p (t h) -> p h t", t=TILES),
                 in1=bias[:, feats].unsqueeze(2).to_broadcast([P, P, PACK]),
                 op=ALU.add,
@@ -186,119 +174,98 @@ def tile_scaleddotproductattention_pa_t_kernel(tc, q, k, x, Wv, bv, out):
 
         def multiply_output(b, m):
             filled["o", b, m] = new_bank()
-            mx_pass(filled["o", b, m][:], operands["e", b], m * P, operands["v", b], 0, H)
+            mx_pass(filled["o", b, m][:], coded["e", b], m * P, coded["v", b], 0, H)
 
-        def divide_and_store(b, m):
-            nc.scalar.activation(
-                out=soft["out", b][:, m, :],
-                in_=filled["o", b, m][:],
-                func=ACT.Copy,
-                scale=soft["inv_sum", b][:, m : m + 1],
-            )
-            nc.sync.dma_start(out=out[b, m * P : (m + 1) * P, :], in_=soft["out", b][:, m, :])
+        def divide_and_store(b, m, on_vector):
+            result = results.tile([P, H], F32, name="result", tag="result")
+            if on_vector:
+                nc.vector.tensor_scalar_mul(
+                    out=result[:], in0=filled["o", b, m][:], scalar1=soft["inv_sum", b][:, m : m + 1]
+                )
+            else:
+                nc.scalar.activation(
+                    out=result[:], in_=filled["o", b, m][:], func=ACT.Copy, scale=soft["inv_sum", b][:, m : m + 1]
+                )
+            nc.sync.dma_start(out=out[b, m * P : (m + 1) * P, :], in_=result[:])
 
-        load_scores_inputs(0)
-        w_raw = load(const, Wv, "w_raw")
-        load_value_input(0)
+        inputs["k", 0] = load(raw, k[0, :, :], "k_raw")
+        inputs["q", 0] = load(raw, q[0, :, :], "q_raw")
+        inputs["w", 0] = load(const, Wv, "w_raw")
+        inputs["x", 0] = load_paired(raw, x[0, :, :], "x_raw")
         bias = const.tile([P, H], BF16, name="bias")
         nc.sync.dma_start(out=bias[:], in_=bv.partition_broadcast(P))
-        for b in range(1, LOADS_AHEAD):
-            load_scores_inputs(b)
-            load_value_input(b)
+        load_entry(1)
 
         identity = const.tile([P, P], F32, name="identity")
         make_identity(nc, identity[:])
-        diag = {
-            "grouped": const.tile([P, 2 * P * PACK], BF16, name="diag_grouped", align_bytes=64),
-            "codes": const.tile([P, 2 * P], U32, name="diag_codes", align_bytes=64),
-            "scales": const.tile([P, 2 * P], U8, name="diag_scales", align_bytes=64),
-        }
-        nc.vector.memset(diag["grouped"][:], 0.0)
-        slots = diag["grouped"][:].rearrange("p (s c t) -> p s c t", s=2, t=PACK)
+        diag_grouped = const.tile([P, 2 * P * PACK], BF16, name="diag_grouped", align_bytes=64)
+        diag = (
+            const.tile([P, 2 * P], U32, name="diag_codes", align_bytes=64),
+            const.tile([P, 2 * P], U8, name="diag_scales", align_bytes=64),
+        )
+        nc.vector.memset(diag_grouped[:], 0.0)
+        slots = diag_grouped[:].rearrange("p (s c t) -> p s c t", s=2, t=PACK)
         nc.vector.tensor_scalar_mul(out=slots[:, 0, :, 0], in0=identity[:], scalar1=-BIG)
         nc.vector.tensor_scalar_mul(out=slots[:, 1, :, 0], in0=identity[:], scalar1=BIG)
-        quantise(diag, 0, 2 * P)
+        nc.vector.quantize_mx(out=diag[0][:].bitcast(FP8X4), scales=diag[1][:], in_=diag_grouped[:])
         zero = const.tile([P, 1], F32, name="zero")
         one = const.tile([P, 1], F32, name="one")
         nc.vector.memset(zero[:], 0.0)
         nc.scalar.activation(out=one[:], in_=zero[:], func=ACT.Exp)
 
-        w_op = mx_operand(const, "w")
-        flip_input("k", 0)
-        flip_input("q", 0)
-        flip(w_raw, w_op, "w")
-        flip_input("x", 0)
-        quantise(operands["k", 0], 0, L)
-        quantise(operands["q", 0], 0, L)
-        multiply_scores(0, 0)
-        quantise(w_op, 0, H)
+        def turned(s):
+            r, j = divmod(s, TILES)
+            if s == W_STEP:
+                return ("w", 0)
+            key = (("k", r + 1), ("q", r + 1), ("e", r - 1), ("x", r + 1))[j]
+            return key if live(key[1]) else None
 
-        for r in range(B + 1):
-            nxt, cur, prv = r + 1, r, r - 1
-            prepare, soften, finish = nxt < B, cur < B, prv >= 0
+        for s in range(FIRST_STEP, LAST_STEP + 1):
+            r, j = divmod(s, TILES)
+            before_r, before_j = divmod(s - 1, TILES)
+            v_entry, v_block = divmod(s - 1, TILES)
+            ends = s < 0 or s > TILES * B
 
-            if r + LOADS_AHEAD < B:
-                load_scores_inputs(r + LOADS_AHEAD)
-                load_value_input(r + LOADS_AHEAD)
+            if j == 0 and live(r + LOADS_AHEAD):
+                load_entry(r + LOADS_AHEAD)
 
-            if soften:
-                soft["a", cur] = work.tile([P, TILES * L], F32, name="a_sb", tag="a_sb")
-                soft["neg_max", cur] = work.tile([P, TILES], F32, name="neg_max", tag="neg_max")
-                take_scores(cur, 0)
-            if finish:
-                quantise(operands["v", prv], 0, H)
-                operands["e", prv] = mx_operand(work, "e")
-                flip(soft["e", prv], operands["e", prv], ("e", prv))
-            if prepare:
-                flip_input("k", nxt)
-            if finish:
-                quantise(operands["e", prv], 0, L // 2)
-                quantise(operands["e", prv], L // 2, L // 2)
-                soft["inv_sum", prv] = work.tile([P, TILES], F32, name="inv_sum", tag="inv_sum")
-                nc.vector.reciprocal(out=soft["inv_sum", prv][:], in_=soft["row_sum", prv][:])
-            if soften:
-                quantise(operands["x", cur], 0, L)
-                multiply_scores(cur, 1)
-            if prepare:
-                flip_input("q", nxt)
-                operands["x", nxt] = mx_operand(work, "x")
-                turn(inputs["x", nxt], ("x", nxt), 0)
-                collect(operands["x", nxt], ("x", nxt), 0, nc.scalar.copy)
-                turn(inputs["x", nxt], ("x", nxt), 1)
-            if soften:
-                take_scores(cur, 1)
-            if prepare:
-                quantise(operands["k", nxt], 0, L)
-            if soften:
-                operands["v", cur] = mx_operand(work, "v")
-                multiply_values(cur, 0)
-                multiply_scores(cur, 2)
-                multiply_values(cur, 1)
-                multiply_scores(cur, 3)
-                multiply_values(cur, 2)
-                multiply_values(cur, 3)
-                add_bias(cur, 0)
-                take_scores(cur, 2)
-                take_scores(cur, 3)
-            if prepare:
-                collect(operands["x", nxt], ("x", nxt), 1, nc.vector.tensor_copy)
-            if soften:
-                add_bias(cur, 1)
-            if prepare:
-                quantise(operands["q", nxt], 0, L)
-            if soften:
-                add_bias(cur, 2)
-                add_bias(cur, 3)
-                soft["e", cur] = work.tile([P, TILES * L], BF16, name="e_sb", tag="e_sb")
-                soft["row_sum", cur] = work.tile([P, TILES], F32, name="row_sum", tag="row_sum")
-                for m in range(TILES):
-                    exponential(cur, m)
-            if finish:
-                for m in range(TILES):
-                    multiply_output(prv, m)
-            if prepare:
-                multiply_scores(nxt, 0)
-            if finish:
-                soft["out", prv] = results.tile([P, TILES, H], F32, name="out_sb", tag="out_sb")
-                for m in range(TILES):
-                    divide_and_store(prv, m)
+            job = turned(s)
+            if job:
+                new_grouped(job)
+                turn(job, 0)
+                turn(job, 1)
+            if live(r):
+                multiply_scores(r, j)
+            if live(v_entry):
+                multiply_values(v_entry, v_block)
+            if live(r - 2):
+                multiply_output(r - 2, j)
+
+            if live(before_r - 2):
+                divide_and_store(before_r - 2, before_j, on_vector=(ends and before_j % 2 == 1))
+            if job:
+                collect(job, 0, nc.scalar.copy)
+                collect(job, 1, nc.vector.tensor_copy if ends or job[0] == "x" else nc.scalar.copy)
+            if live(before_r):
+                if before_j == 0:
+                    inputs["e", before_r] = work.tile([P, TILES * L], BF16, name="e_sb", tag="e_sb")
+                    soft["row_sum", before_r] = work.tile([P, TILES], F32, name="row_sum", tag="row_sum")
+                exponential(before_r, before_j)
+
+            done = turned(s - 1)
+            if done:
+                quantise(done)
+                if done[0] == "e":
+                    soft["inv_sum", done[1]] = work.tile([P, TILES], F32, name="inv_sum", tag="inv_sum")
+                    nc.vector.reciprocal(out=soft["inv_sum", done[1]][:], in_=soft["row_sum", done[1]][:])
+            if j == 1 and live(r - 1):
+                quantise(("v", r - 1))
+            if live(r):
+                if j == 0:
+                    soft["a", r] = work.tile([P, TILES * L], F32, name="a_sb", tag="a_sb")
+                    soft["neg_max", r] = work.tile([P, TILES], F32, name="neg_max", tag="neg_max")
+                take_scores(r, j)
+            if live(v_entry):
+                if v_block == 0:
+                    new_grouped(("v", v_entry))
+                add_bias(v_entry, v_block)

@@ -245,7 +245,7 @@ def tile_scaleddotproductattention_pa_t_kernel(tc, q, k, x, Wv, bv, out):
                 divide_and_store(before_r - 2, before_j, on_vector=(ends and before_j % 2 == 1))
             if job:
                 collect(job, 0, nc.scalar.copy)
-                collect(job, 1, nc.vector.tensor_copy if ends or job[0] == "x" else nc.scalar.copy)
+                collect(job, 1, nc.vector.tensor_copy if ends else nc.scalar.copy)
             if live(before_r):
                 if before_j == 0:
                     inputs["e", before_r] = work.tile([P, TILES * L], BF16, name="e_sb", tag="e_sb")

@@ -192,8 +192,12 @@ def tile_scaleddotproductattention_pa_t_kernel(tc, q, k, x, Wv, bv, out):
         inputs["q", 0] = load(raw, q[0, :, :], "q_raw")
         inputs["w", 0] = load(const, Wv, "w_raw")
         inputs["x", 0] = load_paired(raw, x[0, :, :], "x_raw")
+        bias_row = const.tile([P, H], BF16, name="bias_row")
+        ones = const.tile([P, P], BF16, name="ones")
         bias = const.tile([P, H], BF16, name="bias")
-        nc.sync.dma_start(out=bias[:], in_=bv.partition_broadcast(P))
+        nc.vector.memset(bias_row[:], 0.0)
+        nc.vector.memset(ones[:], 1.0)
+        nc.sync.dma_start(out=bias_row[0:1, :], in_=bv.rearrange("(o h) -> o h", o=1))
         load_entry(1)
 
         identity = const.tile([P, P], F32, name="identity")
@@ -234,6 +238,9 @@ def tile_scaleddotproductattention_pa_t_kernel(tc, q, k, x, Wv, bv, out):
                 new_grouped(job)
                 turn(job, 0)
                 turn(job, 1)
+            if s == W_STEP:
+                bias_bank = new_bank()
+                nc.tensor.matmul(out=bias_bank[:], lhsT=ones[:], rhs=bias_row[:], start=True, stop=True)
             if live(r):
                 multiply_scores(r, j)
             if live(v_entry):
@@ -258,6 +265,8 @@ def tile_scaleddotproductattention_pa_t_kernel(tc, q, k, x, Wv, bv, out):
                 if done[0] == "e":
                     soft["inv_sum", done[1]] = work.tile([P, TILES], F32, name="inv_sum", tag="inv_sum")
                     nc.vector.reciprocal(out=soft["inv_sum", done[1]][:], in_=soft["row_sum", done[1]][:])
+            if s == W_STEP:
+                nc.vector.tensor_copy(out=bias[:], in_=bias_bank[:])
             if j == 1 and live(r - 1):
                 quantise(("v", r - 1))
             if live(r):

@@ -252,7 +252,8 @@ def tile_scaleddotproductattention_pa_t_kernel(tc, q, k, x, Wv, bv, out):
                 divide_and_store(before_r - 2, before_j, on_vector=(ends and before_j % 2 == 1))
             if job:
                 collect(job, 0, nc.scalar.copy)
-                collect(job, 1, nc.vector.tensor_copy if ends else nc.scalar.copy)
+                shared = ends or (job[0] == "x" and r >= B // 2)
+                collect(job, 1, nc.vector.tensor_copy if shared else nc.scalar.copy)
             if live(before_r):
                 if before_j == 0:
                     inputs["e", before_r] = work.tile([P, TILES * L], BF16, name="e_sb", tag="e_sb")

from contextlib import ExitStack

import concourse.mybir as mybir
from concourse.masks import make_identity

F32 = mybir.dt.float32
BF16 = mybir.dt.bfloat16
U32 = mybir.dt.uint32
U8 = mybir.dt.uint8
FP8X4 = mybir.dt.float8_e4m3fn_x4
ALU = mybir.AluOpType
ACT = mybir.ActivationFunctionType

P = 128
PACK = 4
B, L, H = 8, 512, 512
TILES = L // P
BANK = 512
PSUM_BANKS = 8
BIG = 2.0**60
LOADS_AHEAD = 3
FIRST_STEP = -TILES
W_STEP = -2
LAST_STEP = TILES * (B + 2)

FLOPS = 3 * 2 * B * L * H * H


def sides(m):
    return [(first, last) for first, last in ((0, m * P), ((m + 1) * P, L)) if first < last]


def passes(first, last):
    cuts = []
    while first < last:
        count = min(2 * P, last - first)
        cuts.append((first, count))
        first += count
    return cuts


def tile_scaleddotproductattention_pa_t_kernel(tc, q, k, x, Wv, bv, out):
    nc = tc.nc
    with ExitStack() as ctx:
        const = ctx.enter_context(tc.tile_pool(name="const", bufs=1))
        raw = ctx.enter_context(tc.tile_pool(name="raw", bufs=LOADS_AHEAD + 1))
        work = ctx.enter_context(tc.tile_pool(name="work", bufs=2))
        results = ctx.enter_context(tc.tile_pool(name="results", bufs=6))
        banks = ctx.enter_context(tc.psum_pool(name="banks", bufs=PSUM_BANKS))
        ctx.enter_context(tc.manual_schedule())

        inputs = {}
        grouped = {}
        coded = {}
        soft = {}
        filled = {}

        def live(b):
            return 0 <= b < B

        def new_bank():
            return banks.tile([P, BANK], F32, name="bank", tag="bank")

        def load(pool, rows, name):
            tile = pool.tile([P, TILES * H], BF16, name=name, tag=name)
            nc.sync.dma_start(
                out=tile[:].rearrange("p (s f) -> p s f", s=TILES),
                in_=rows.rearrange("(s p) f -> p s f", p=P),
            )
            return tile

        def load_paired(pool, rows, name):
            tile = pool.tile([P, TILES * H], BF16, name=name, tag=name)
            nc.sync.dma_start(
                out=tile[:].rearrange("p (u e f) -> p u e f", u=2, e=2),
                in_=rows.rearrange("(u p e) f -> p u e f", u=2, e=2),
            )
            return tile

        def load_entry(b):
            inputs["k", b] = load(raw, k[b, :, :], "k_raw")
            inputs["q", b] = load(raw, q[b, :, :], "q_raw")
            inputs["x", b] = load_paired(raw, x[b, :, :], "x_raw")

        def new_grouped(key):
            name = key[0] + "_grouped"
            grouped[key] = work.tile([P, L * PACK], BF16, name=name, tag=name, align_bytes=64)

        def turn(key, half):
            words = inputs[key][:].bitcast(F32).rearrange("p (s w) -> p s w", s=TILES)
            filled["t", key, half] = new_bank()
            planes = filled["t", key, half][:].rearrange("p (u c) -> p u c", u=2)
            for s in range(2):
                for u in range(2):
                    nc.tensor.transpose(
                        planes[:, u, s * P : (s + 1) * P],
                        words[:, 2 * half + s, u * P : (u + 1) * P],
                        identity[:],
                    )

        def collect(key, half, copy):
            pairs = grouped[key][:].bitcast(F32).rearrange("p (c u) -> p c u", u=2)
            planes = filled["t", key, half][:].rearrange("p (u c) -> p u c", u=2)
            copy(
                out=pairs[:, half * 2 * P : (half + 1) * 2 * P, :],
                in_=planes.rearrange("p u c -> p c u"),
            )

        def quantise(key):
            name = key[0]
            codes = work.tile([P, L], U32, name=name + "_codes", tag=name + "_codes", align_bytes=64)
            scales = work.tile([P, L], U8, name=name + "_scales", tag=name + "_scales", align_bytes=64)
            nc.vector.quantize_mx(out=codes[:].bitcast(FP8X4), scales=scales[:], in_=grouped[key][:])
            coded[key] = (codes, scales)

        def mx_pass(acc, stationary, s_first, moving, m_first, m_count, start=True, stop=True):
            s_cols = slice(s_first, s_first + P)
            m_cols = slice(m_first, m_first + m_count)
            nc.tensor.matmul_mx(
                out=acc,
                lhsT=stationary[0][:, s_cols].bitcast(FP8X4),
                lhsT_scale=stationary[1][:, s_cols],
                rhs=moving[0][:, m_cols].bitcast(FP8X4),
                rhs_scale=moving[1][:, m_cols],
                start=start,
                stop=stop,
            )

        def multiply_scores(b, m):
            filled["s", b, m] = new_bank()
            bank = filled["s", b, m]
            for first, last in sides(m):
                for start, count in passes(first, last):
                    mx_pass(bank[:, start : start + count], coded["q", b], m * P, coded["k", b], start, count)
            own = bank[:, m * P : (m + 1) * P]
            mx_pass(own, coded["q", b], m * P, coded["k", b], m * P, P, start=True, stop=False)
            mx_pass(own, diag, 0, diag, P, P, start=False, stop=True)

        def take_scores(b, m):
            nc.vector.tensor_scalar(
                out=soft["a", b][:, m * L : (m + 1) * L],
                in0=filled["s", b, m][:],
                scalar1=-1.0 / H,
                scalar2=None,
                op0=ALU.mult,
                op1=ALU.min,
                accum_out=soft["neg_max", b][:, m : m + 1],
            )

        def exponential(b, m):
            nc.scalar.activation(
                out=inputs["e", b][:, m * L : (m + 1) * L],
                in_=soft["a", b][:, m * L : (m + 1) * L],
                func=ACT.Exp,
                bias=soft["neg_max", b][:, m : m + 1],
                scale=-1.0,
                accum_out=soft["row_sum", b][:, m : m + 1],
            )

        def multiply_values(b, c):
            filled["v", b, c] = new_bank()
            tiles = filled["v", b, c][:].rearrange("p (t h) -> p t h", t=TILES)
            for t in range(TILES):
                mx_pass(tiles[:, t, :], coded["x", b], t * P, coded["w", 0], c * P, P)

        def add_bias(b, c):
            feats = slice(c * P, (c + 1) * P)
            nc.vector.tensor_tensor(
                out=grouped["v", b][:].rearrange("p (h t) -> p h t", t=PACK)[:, feats, :],
                in0=filled["v", b, c][:].rearrange("p (t h) -> p h t", t=TILES),
                in1=bias[:, feats].unsqueeze(2).to_broadcast([P, P, PACK]),
                op=ALU.add,
            )

        def multiply_output(b, m):
            filled["o", b, m] = new_bank()
            mx_pass(filled["o", b, m][:], coded["e", b], m * P, coded["v", b], 0, H)

        def divide_and_store(b, m, on_vector):
            result = results.tile([P, H], F32, name="result", tag="result")
            if on_vector:
                nc.vector.tensor_scalar_mul(
                    out=result[:], in0=filled["o", b, m][:], scalar1=soft["inv_sum", b][:, m : m + 1]
                )
            else:
                nc.scalar.activation(
                    out=result[:], in_=filled["o", b, m][:], func=ACT.Copy, scale=soft["inv_sum", b][:, m : m + 1]
                )
            nc.sync.dma_start(out=out[b, m * P : (m + 1) * P, :], in_=result[:])

        inputs["k", 0] = load(raw, k[0, :, :], "k_raw")
        inputs["q", 0] = load(raw, q[0, :, :], "q_raw")
        inputs["w", 0] = load(const, Wv, "w_raw")
        inputs["x", 0] = load_paired(raw, x[0, :, :], "x_raw")
        bias_row = const.tile([P, H], BF16, name="bias_row")
        ones = const.tile([P, P], BF16, name="ones")
        bias = const.tile([P, H], BF16, name="bias")
        nc.vector.memset(bias_row[:], 0.0)
        nc.vector.memset(ones[:], 1.0)
        nc.sync.dma_start(out=bias_row[0:1, :], in_=bv.rearrange("(o h) -> o h", o=1))
        load_entry(1)

        identity = const.tile([P, P], F32, name="identity")
        make_identity(nc, identity[:])
        diag_grouped = const.tile([P, 2 * P * PACK], BF16, name="diag_grouped", align_bytes=64)
        diag = (
            const.tile([P, 2 * P], U32, name="diag_codes", align_bytes=64),
            const.tile([P, 2 * P], U8, name="diag_scales", align_bytes=64),
        )
        nc.vector.memset(diag_grouped[:], 0.0)
        slots = diag_grouped[:].rearrange("p (s c t) -> p s c t", s=2, t=PACK)
        nc.vector.tensor_scalar_mul(out=slots[:, 0, :, 0], in0=identity[:], scalar1=-BIG)
        nc.vector.tensor_scalar_mul(out=slots[:, 1, :, 0], in0=identity[:], scalar1=BIG)
        nc.vector.quantize_mx(out=diag[0][:].bitcast(FP8X4), scales=diag[1][:], in_=diag_grouped[:])
        zero = const.tile([P, 1], F32, name="zero")
        one = const.tile([P, 1], F32, name="one")
        nc.vector.memset(zero[:], 0.0)
        nc.scalar.activation(out=one[:], in_=zero[:], func=ACT.Exp)

        def turned(s):
            r, j = divmod(s, TILES)
            if s == W_STEP:
                return ("w", 0)
            key = (("k", r + 1), ("q", r + 1), ("e", r - 1), ("x", r + 1))[j]
            return key if live(key[1]) else None

        for s in range(FIRST_STEP, LAST_STEP + 1):
            r, j = divmod(s, TILES)
            before_r, before_j = divmod(s - 1, TILES)
            v_entry, v_block = divmod(s - 1, TILES)
            ends = s < 0 or s > TILES * B

            if j == 0 and live(r + LOADS_AHEAD):
                load_entry(r + LOADS_AHEAD)

            job = turned(s)
            if job:
                new_grouped(job)
                turn(job, 0)
                turn(job, 1)
            if s == W_STEP:
                bias_bank = new_bank()
                nc.tensor.matmul(out=bias_bank[:], lhsT=ones[:], rhs=bias_row[:], start=True, stop=True)
            if live(r):
                multiply_scores(r, j)
            if live(v_entry):
                multiply_values(v_entry, v_block)
            if live(r - 2):
                multiply_output(r - 2, j)

            if live(before_r - 2):
                divide_and_store(before_r - 2, before_j, on_vector=(ends and before_j % 2 == 1))
            if job:
                collect(job, 0, nc.scalar.copy)
                shared = ends or (job[0] == "x" and r >= B // 2)
                collect(job, 1, nc.vector.tensor_copy if shared else nc.scalar.copy)
            if live(before_r):
                if before_j == 0:
                    inputs["e", before_r] = work.tile([P, TILES * L], BF16, name="e_sb", tag="e_sb")
                    soft["row_sum", before_r] = work.tile([P, TILES], F32, name="row_sum", tag="row_sum")
                exponential(before_r, before_j)

            done = turned(s - 1)
            if done:
                quantise(done)
                if done[0] == "e":
                    soft["inv_sum", done[1]] = work.tile([P, TILES], F32, name="inv_sum", tag="inv_sum")
                    nc.vector.reciprocal(out=soft["inv_sum", done[1]][:], in_=soft["row_sum", done[1]][:])
            if s == W_STEP:
                nc.vector.tensor_copy(out=bias[:], in_=bias_bank[:])
            if j == 1 and live(r - 1):
                quantise(("v", r - 1))
            if live(r):
                if j == 0:
                    soft["a", r] = work.tile([P, TILES * L], F32, name="a_sb", tag="a_sb")
                    soft["neg_max", r] = work.tile([P, TILES], F32, name="neg_max", tag="neg_max")
                take_scores(r, j)
            if live(v_entry):
                if v_block == 0:
                    new_grouped(("v", v_entry))
                add_bias(v_entry, v_block)
